import numpy as np
import ml_dtypes


def mxq(x, axis, fmt="e4m3"):
    dtype, down = {"e4m3": (ml_dtypes.float8_e4m3fn, 7), "e5m2": (ml_dtypes.float8_e5m2, 14)}[fmt]
    v = np.moveaxis(np.asarray(x, np.float32).astype(ml_dtypes.bfloat16).astype(np.float64), axis, -1)
    blocks = v.reshape(v.shape[:-1] + (-1, 32))
    amax = np.abs(blocks).max(-1, keepdims=True)
    byte = np.maximum(np.where(amax > 0, np.frexp(amax)[1] - 1 + 127, 0) - down, 1)
    scale = np.exp2(byte - 127.0)
    codes = (blocks / scale).astype(np.float32).astype(dtype).astype(np.float64)
    return np.moveaxis((codes * scale).reshape(v.shape), -1, axis)


WIDE = False


def mx_kscale(k):
    if not WIDE:
        return np.ones(k)
    levels = np.array([10, -10, 5, -5, 0])
    a = np.random.permutation(np.resize(levels, k // 512 * 4)).reshape(k // 512, 4)
    idx = np.arange(k)
    return np.exp2(a[idx // 512, idx % 128 // 32])


BF16 = ml_dtypes.bfloat16


def bf(x):
    return np.asarray(x, np.float32).astype(BF16)


def f64(x):
    return np.asarray(x).astype(np.float64)


B, S, D, H = 1, 512, 1024, 8
DK = D // H


def setup_inputs():
    u = mx_kscale(S)
    r = u / u.max()
    return {"f0": bf(np.random.standard_normal((B, H, S, DK)) * r[:, None]),
            "f1": bf(np.random.standard_normal((B, H, S, DK)) * r[:, None]),
            "wo": bf(np.random.standard_normal((D, S)) / np.sqrt(S) / r[None, :]),
            "bo": bf(np.random.standard_normal(D) * 0.3)}


def reference(f0, f1, wo, bo):
    scale = 1.0 / np.sqrt(DK)
    f0, f1 = f64(f0), f64(f1)
    comb = (f0 @ f1.transpose(0, 1, 3, 2) + f1 @ f0.transpose(0, 1, 3, 2)) * (scale * 0.5)
    return (mxq(comb, 3, "e4m3") @ mxq(f64(wo), 1, "e4m3").T) + f64(bo)

@@ -1,0 +1,211 @@
+import math
+from contextlib import ExitStack
+
+import concourse.mybir as mybir
+from concourse.masks import make_identity
+
+BF16 = mybir.dt.bfloat16
+F32 = mybir.dt.float32
+U32 = mybir.dt.uint32
+U8 = mybir.dt.uint8
+FP8X4 = mybir.dt.float8_e4m3fn_x4
+
+P = 128
+PACK = 4
+HEADS = 8
+TOKENS = 512
+HEAD_DIM = 128
+FEATURES = 1024
+N_TILE = 512
+N_TILES = FEATURES // N_TILE
+WO_ROW_TILES = FEATURES // P
+WORDS = 2
+BLOCKS = HEADS * PACK
+BLOCKS_PER_STORE = 2
+COMB_SCALE = 0.5 / math.sqrt(HEAD_DIM)
+
+QUANTISE_LAG = 1
+PROJECT_LAG = 2
+TRANSPOSE_AT = 2
+
+FLOPS = 2 * HEADS * TOKENS * TOKENS * (2 * HEAD_DIM + FEATURES)
+
+
+def tile_multimodalmutualattention_pb_kernel(tc, f0, f1, wo, bo, out):
+    nc = tc.nc
+    with ExitStack() as ctx:
+        const = ctx.enter_context(tc.tile_pool(name="const", bufs=1))
+        ft_pool = ctx.enter_context(tc.tile_pool(name="ft", bufs=2))
+        mx_pool = ctx.enter_context(tc.tile_pool(name="mx", bufs=4))
+        out_pool = ctx.enter_context(tc.tile_pool(name="outs", bufs=4))
+        psum_t = ctx.enter_context(tc.psum_pool(name="psum_t", bufs=1))
+        psum_c = ctx.enter_context(tc.psum_pool(name="psum_c", bufs=3))
+        psum_o = ctx.enter_context(tc.psum_pool(name="psum_o", bufs=4))
+        ctx.enter_context(tc.manual_schedule())
+
+        ident_bf16 = const.tile([P, P], BF16)
+        make_identity(nc, ident_bf16[:])
+        ident_f32 = const.tile([P, P], F32)
+        make_identity(nc, ident_f32[:])
+        ones = const.tile([P, P], BF16)
+        nc.vector.memset(ones[:], 1.0)
+        bo_rows = const.tile([P, FEATURES], BF16)
+        nc.vector.memset(bo_rows[:], 0.0)
+        nc.scalar.dma_start(out=bo_rows[0:1, :], in_=bo.rearrange("(o d) -> o d", o=1))
+
+        f0_sb = const.tile([P, HEADS, PACK * HEAD_DIM], BF16)
+        f1_sb = const.tile([P, HEADS, PACK * HEAD_DIM], BF16)
+        f_sb = (f0_sb, f1_sb)
+
+        def load_heads(first, last):
+            for f_dram, f_tile in zip((f0, f1), f_sb):
+                nc.sync.dma_start(
+                    out=f_tile[:, first:last, :],
+                    in_=f_dram[0, first:last].rearrange("h (p j) d -> p h (j d)", j=PACK),
+                )
+
+        wo_sb = const.tile([P, WO_ROW_TILES * TOKENS], BF16)
+        wo_sb_tiles = wo_sb[:].rearrange("r (b t) -> r b t", t=TOKENS)
+        wo_dram_tiles = wo.rearrange("(b r) t -> r b t", r=P)
+        tiles_per_half = WO_ROW_TILES // N_TILES
+
+        load_heads(0, 1)
+        for n in range(N_TILES):
+            b_range = slice(n * tiles_per_half, (n + 1) * tiles_per_half)
+            nc.sync.dma_start(out=wo_sb_tiles[:, b_range, :], in_=wo_dram_tiles[:, b_range, :])
+        load_heads(1, HEADS)
+
+        bias = const.tile([P, FEATURES], F32)
+        for n in range(N_TILES):
+            n_cols = slice(n * N_TILE, (n + 1) * N_TILE)
+            acc = psum_o.tile([P, N_TILE], F32)
+            nc.tensor.matmul(acc[:], lhsT=ones[:], rhs=bo_rows[:, n_cols], start=True, stop=True)
+            nc.vector.tensor_copy(out=bias[:, n_cols], in_=acc[:])
+
+        def transpose_head(h):
+            tp = psum_t.tile([P, 2, TOKENS], BF16)
+            for source in range(2):
+                for j in range(PACK):
+                    nc.tensor.transpose(
+                        tp[:, source, j * P : (j + 1) * P],
+                        f_sb[source][:, h, j * HEAD_DIM : (j + 1) * HEAD_DIM],
+                        ident_bf16[:],
+                    )
+            fT = ft_pool.tile([P, 2, TOKENS], BF16)
+            nc.scalar.copy(out=fT[:], in_=tp[:])
+            return fT
+
+        def comb_group(fT, bank, j, jc):
+            rows = slice(j * P, (j + 1) * P)
+            cols = slice(jc * P, (jc + 1) * P)
+            nc.tensor.matmul(
+                bank[:, j, :], lhsT=fT[:, 0, rows], rhs=fT[:, 1, cols], start=True, stop=False
+            )
+            nc.tensor.matmul(
+                bank[:, j, :], lhsT=fT[:, 1, rows], rhs=fT[:, 0, cols], start=False, stop=True
+            )
+
+        fT_of_head = {0: transpose_head(0)}
+
+        wo_words = wo_sb[:].bitcast(F32).rearrange("r (b p u) -> r b u p", b=WO_ROW_TILES, u=WORDS)
+        wo_grouped = const.tile([P, FEATURES * PACK], BF16, align_bytes=64)
+        wo_grouped_words = wo_grouped[:].bitcast(F32).rearrange(
+            "p (b r u) -> p b r u", b=WO_ROW_TILES, u=WORDS
+        )
+        wo_codes = const.tile([P, FEATURES], U32, align_bytes=64)
+        wo_scales = const.tile([P, FEATURES], U8, align_bytes=64)
+        tiles_per_bank = N_TILE // (WORDS * P)
+        for n in range(N_TILES):
+            for first_b in range(n * tiles_per_half, (n + 1) * tiles_per_half, tiles_per_bank):
+                bank = psum_c.tile([P, tiles_per_bank, WORDS, P], F32, tag="bank")
+                for i in range(tiles_per_bank):
+                    for u in range(WORDS):
+                        nc.tensor.transpose(
+                            bank[:, i, u, :], wo_words[:, first_b + i, u, :], ident_f32[:]
+                        )
+                nc.vector.tensor_copy(
+                    out=wo_grouped_words[:, first_b : first_b + tiles_per_bank, :, :],
+                    in_=bank[:].rearrange("p i u r -> p i r u"),
+                )
+            nc.vector.quantize_mx(
+                out=wo_codes[:, n * N_TILE : (n + 1) * N_TILE].bitcast(FP8X4),
+                scales=wo_scales[:, n * N_TILE : (n + 1) * N_TILE],
+                in_=wo_grouped[:, n * N_TILE * PACK : (n + 1) * N_TILE * PACK],
+            )
+
+        grouped_of_block = {}
+        codes_of_block = {}
+        scales_of_block = {}
+        result_of_store = {}
+
+        def make_comb(block):
+            h, jc = divmod(block, PACK)
+            fT = fT_of_head[h]
+            bank = psum_c.tile([P, PACK, P], F32, tag="bank")
+            for j in range(PACK // 2):
+                comb_group(fT, bank, j, jc)
+            if jc == TRANSPOSE_AT and h + 1 < HEADS:
+                fT_of_head[h + 1] = transpose_head(h + 1)
+            for j in range(PACK // 2, PACK):
+                comb_group(fT, bank, j, jc)
+            grouped = mx_pool.tile([P, P, PACK], BF16, align_bytes=64)
+            nc.scalar.activation(
+                out=grouped[:],
+                in_=bank[:].rearrange("p j c -> p c j"),
+                func=mybir.ActivationFunctionType.Copy,
+                scale=COMB_SCALE,
+            )
+            grouped_of_block[block] = grouped
+
+        def quantise(block):
+            codes = mx_pool.tile([P, P], U32, align_bytes=64)
+            scales = mx_pool.tile([P, P], U8, align_bytes=64)
+            nc.vector.quantize_mx(
+                out=codes[:].bitcast(FP8X4),
+                scales=scales[:],
+                in_=grouped_of_block[block][:].rearrange("p c j -> p (c j)"),
+            )
+            codes_of_block[block] = codes
+            scales_of_block[block] = scales
+
+        def project(block):
+            h, jc = divmod(block, PACK)
+            store, place = divmod(block, BLOCKS_PER_STORE)
+            if place == 0:
+                result = out_pool.tile([P, BLOCKS_PER_STORE, FEATURES], F32)
+                result_of_store[store] = result
+            result = result_of_store[store]
+            for n in range(N_TILES):
+                n_cols = slice(n * N_TILE, (n + 1) * N_TILE)
+                acc = psum_o.tile([P, N_TILE], F32)
+                nc.tensor.matmul_mx(
+                    out=acc[:],
+                    lhsT=codes_of_block[block][:].bitcast(FP8X4),
+                    lhsT_scale=scales_of_block[block][:],
+                    rhs=wo_codes[:, n_cols].bitcast(FP8X4),
+                    rhs_scale=wo_scales[:, n_cols],
+                    start=True,
+                    stop=True,
+                )
+                nc.vector.tensor_tensor(
+                    out=result[:, place, n_cols],
+                    in0=acc[:],
+                    in1=bias[:, n_cols],
+                    op=mybir.AluOpType.add,
+                )
+            if place == BLOCKS_PER_STORE - 1:
+                first_jc = jc - place
+                nc.sync.dma_start(
+                    out=out[0, h].rearrange("(c j) d -> c j d", j=PACK)[
+                        :, first_jc : first_jc + BLOCKS_PER_STORE, :
+                    ],
+                    in_=result[:],
+                )
+
+        for step in range(BLOCKS + PROJECT_LAG):
+            if step < BLOCKS:
+                make_comb(step)
+            if 0 <= step - QUANTISE_LAG < BLOCKS:
+                quantise(step - QUANTISE_LAG)
+            if 0 <= step - PROJECT_LAG:
+                project(step - PROJECT_LAG)

@@ -21,12 +21,14 @@ N_TILES = FEATURES // N_TILE
 WO_ROW_TILES = FEATURES // P
 WORDS = 2
 BLOCKS = HEADS * PACK
-BLOCKS_PER_STORE = 2
+BLOCKS_PER_STORE = 1
 COMB_SCALE = 0.5 / math.sqrt(HEAD_DIM)
 
 QUANTISE_LAG = 1
 PROJECT_LAG = 2
-TRANSPOSE_AT = 2
+TRANSPOSE_AT = 1
+
+BANKS_PER_DETOUR = 4
 
 FLOPS = 2 * HEADS * TOKENS * TOKENS * (2 * HEAD_DIM + FEATURES)
 
@@ -37,7 +39,7 @@ def tile_multimodalmutualattention_pb_kernel(tc, f0, f1, wo, bo, out):
         const = ctx.enter_context(tc.tile_pool(name="const", bufs=1))
         ft_pool = ctx.enter_context(tc.tile_pool(name="ft", bufs=2))
         mx_pool = ctx.enter_context(tc.tile_pool(name="mx", bufs=4))
-        out_pool = ctx.enter_context(tc.tile_pool(name="outs", bufs=4))
+        out_pool = ctx.enter_context(tc.tile_pool(name="outs", bufs=6))
         psum_t = ctx.enter_context(tc.psum_pool(name="psum_t", bufs=1))
         psum_c = ctx.enter_context(tc.psum_pool(name="psum_c", bufs=3))
         psum_o = ctx.enter_context(tc.psum_pool(name="psum_o", bufs=4))
@@ -47,11 +49,10 @@ def tile_multimodalmutualattention_pb_kernel(tc, f0, f1, wo, bo, out):
         make_identity(nc, ident_bf16[:])
         ident_f32 = const.tile([P, P], F32)
         make_identity(nc, ident_f32[:])
-        ones = const.tile([P, P], BF16)
-        nc.vector.memset(ones[:], 1.0)
         bo_rows = const.tile([P, FEATURES], BF16)
         nc.vector.memset(bo_rows[:], 0.0)
-        nc.scalar.dma_start(out=bo_rows[0:1, :], in_=bo.rearrange("(o d) -> o d", o=1))
+        ones = const.tile([P, P], BF16)
+        nc.vector.memset(ones[:], 1.0)
 
         f0_sb = const.tile([P, HEADS, PACK * HEAD_DIM], BF16)
         f1_sb = const.tile([P, HEADS, PACK * HEAD_DIM], BF16)
@@ -73,14 +74,9 @@ def tile_multimodalmutualattention_pb_kernel(tc, f0, f1, wo, bo, out):
         for n in range(N_TILES):
             b_range = slice(n * tiles_per_half, (n + 1) * tiles_per_half)
             nc.sync.dma_start(out=wo_sb_tiles[:, b_range, :], in_=wo_dram_tiles[:, b_range, :])
-        load_heads(1, HEADS)
-
-        bias = const.tile([P, FEATURES], F32)
-        for n in range(N_TILES):
-            n_cols = slice(n * N_TILE, (n + 1) * N_TILE)
-            acc = psum_o.tile([P, N_TILE], F32)
-            nc.tensor.matmul(acc[:], lhsT=ones[:], rhs=bo_rows[:, n_cols], start=True, stop=True)
-            nc.vector.tensor_copy(out=bias[:, n_cols], in_=acc[:])
+        nc.sync.dma_start(out=bo_rows[0:1, :], in_=bo.rearrange("(o d) -> o d", o=1))
+        load_heads(1, 2)
+        load_heads(2, HEADS)
 
         def transpose_head(h):
             tp = psum_t.tile([P, 2, TOKENS], BF16)
@@ -91,6 +87,9 @@ def tile_multimodalmutualattention_pb_kernel(tc, f0, f1, wo, bo, out):
                         f_sb[source][:, h, j * HEAD_DIM : (j + 1) * HEAD_DIM],
                         ident_bf16[:],
                     )
+            return tp
+
+        def keep_transposed_head(tp):
             fT = ft_pool.tile([P, 2, TOKENS], BF16)
             nc.scalar.copy(out=fT[:], in_=tp[:])
             return fT
@@ -105,7 +104,7 @@ def tile_multimodalmutualattention_pb_kernel(tc, f0, f1, wo, bo, out):
                 bank[:, j, :], lhsT=fT[:, 1, rows], rhs=fT[:, 0, cols], start=False, stop=True
             )
 
-        fT_of_head = {0: transpose_head(0)}
+        fT_of_head = {0: keep_transposed_head(transpose_head(0))}
 
         wo_words = wo_sb[:].bitcast(F32).rearrange("r (b p u) -> r b u p", b=WO_ROW_TILES, u=WORDS)
         wo_grouped = const.tile([P, FEATURES * PACK], BF16, align_bytes=64)
@@ -133,6 +132,13 @@ def tile_multimodalmutualattention_pb_kernel(tc, f0, f1, wo, bo, out):
                 in_=wo_grouped[:, n * N_TILE * PACK : (n + 1) * N_TILE * PACK],
             )
 
+        bias = const.tile([P, FEATURES], F32)
+        for n in range(N_TILES):
+            n_cols = slice(n * N_TILE, (n + 1) * N_TILE)
+            acc = psum_o.tile([P, N_TILE], F32)
+            nc.tensor.matmul(acc[:], lhsT=ones[:], rhs=bo_rows[:, n_cols], start=True, stop=True)
+            nc.vector.tensor_copy(out=bias[:, n_cols], in_=acc[:])
+
         grouped_of_block = {}
         codes_of_block = {}
         scales_of_block = {}
@@ -144,8 +150,9 @@ def tile_multimodalmutualattention_pb_kernel(tc, f0, f1, wo, bo, out):
             bank = psum_c.tile([P, PACK, P], F32, tag="bank")
             for j in range(PACK // 2):
                 comb_group(fT, bank, j, jc)
-            if jc == TRANSPOSE_AT and h + 1 < HEADS:
-                fT_of_head[h + 1] = transpose_head(h + 1)
+            transposes_here = jc == TRANSPOSE_AT and h + 1 < HEADS
+            if transposes_here:
+                tp = transpose_head(h + 1)
             for j in range(PACK // 2, PACK):
                 comb_group(fT, bank, j, jc)
             grouped = mx_pool.tile([P, P, PACK], BF16, align_bytes=64)
@@ -156,6 +163,8 @@ def tile_multimodalmutualattention_pb_kernel(tc, f0, f1, wo, bo, out):
                 scale=COMB_SCALE,
             )
             grouped_of_block[block] = grouped
+            if transposes_here:
+                fT_of_head[h + 1] = keep_transposed_head(tp)
 
         def quantise(block):
             codes = mx_pool.tile([P, P], U32, align_bytes=64)
@@ -187,12 +196,21 @@ def tile_multimodalmutualattention_pb_kernel(tc, f0, f1, wo, bo, out):
                     start=True,
                     stop=True,
                 )
-                nc.vector.tensor_tensor(
-                    out=result[:, place, n_cols],
-                    in0=acc[:],
-                    in1=bias[:, n_cols],
-                    op=mybir.AluOpType.add,
-                )
+                if (block * N_TILES + n) % BANKS_PER_DETOUR == 0:
+                    nc.scalar.copy(out=result[:, place, n_cols], in_=acc[:])
+                    nc.gpsimd.tensor_tensor(
+                        out=result[:, place, n_cols],
+                        in0=result[:, place, n_cols],
+                        in1=bias[:, n_cols],
+                        op=mybir.AluOpType.add,
+                    )
+                else:
+                    nc.vector.tensor_tensor(
+                        out=result[:, place, n_cols],
+                        in0=acc[:],
+                        in1=bias[:, n_cols],
+                        op=mybir.AluOpType.add,
+                    )
             if place == BLOCKS_PER_STORE - 1:
                 first_jc = jc - place
                 nc.sync.dma_start(

@@ -26,6 +26,7 @@ COMB_SCALE = 0.5 / math.sqrt(HEAD_DIM)
 
 QUANTISE_LAG = 1
 PROJECT_LAG = 2
+assert PROJECT_LAG >= N_TILES
 TRANSPOSE_AT = 1
 
 BANKS_PER_DETOUR = 4
@@ -71,10 +72,10 @@ def tile_multimodalmutualattention_pb_kernel(tc, f0, f1, wo, bo, out):
         tiles_per_half = WO_ROW_TILES // N_TILES
 
         load_heads(0, 1)
+        nc.sync.dma_start(out=bo_rows[0:1, :], in_=bo.rearrange("(o d) -> o d", o=1))
         for n in range(N_TILES):
             b_range = slice(n * tiles_per_half, (n + 1) * tiles_per_half)
             nc.sync.dma_start(out=wo_sb_tiles[:, b_range, :], in_=wo_dram_tiles[:, b_range, :])
-        nc.sync.dma_start(out=bo_rows[0:1, :], in_=bo.rearrange("(o d) -> o d", o=1))
         load_heads(1, 2)
         load_heads(2, HEADS)
 
@@ -106,6 +107,13 @@ def tile_multimodalmutualattention_pb_kernel(tc, f0, f1, wo, bo, out):
 
         fT_of_head = {0: keep_transposed_head(transpose_head(0))}
 
+        bias = const.tile([P, FEATURES], F32)
+        for n in range(N_TILES):
+            n_cols = slice(n * N_TILE, (n + 1) * N_TILE)
+            acc = psum_o.tile([P, N_TILE], F32)
+            nc.tensor.matmul(acc[:], lhsT=ones[:], rhs=bo_rows[:, n_cols], start=True, stop=True)
+            nc.vector.tensor_copy(out=bias[:, n_cols], in_=acc[:])
+
         wo_words = wo_sb[:].bitcast(F32).rearrange("r (b p u) -> r b u p", b=WO_ROW_TILES, u=WORDS)
         wo_grouped = const.tile([P, FEATURES * PACK], BF16, align_bytes=64)
         wo_grouped_words = wo_grouped[:].bitcast(F32).rearrange(
@@ -114,7 +122,8 @@ def tile_multimodalmutualattention_pb_kernel(tc, f0, f1, wo, bo, out):
         wo_codes = const.tile([P, FEATURES], U32, align_bytes=64)
         wo_scales = const.tile([P, FEATURES], U8, align_bytes=64)
         tiles_per_bank = N_TILE // (WORDS * P)
-        for n in range(N_TILES):
+
+        def prepare_wo(n):
             for first_b in range(n * tiles_per_half, (n + 1) * tiles_per_half, tiles_per_bank):
                 bank = psum_c.tile([P, tiles_per_bank, WORDS, P], F32, tag="bank")
                 for i in range(tiles_per_bank):
@@ -131,13 +140,6 @@ def tile_multimodalmutualattention_pb_kernel(tc, f0, f1, wo, bo, out):
                 scales=wo_scales[:, n * N_TILE : (n + 1) * N_TILE],
                 in_=wo_grouped[:, n * N_TILE * PACK : (n + 1) * N_TILE * PACK],
             )
-
-        bias = const.tile([P, FEATURES], F32)
-        for n in range(N_TILES):
-            n_cols = slice(n * N_TILE, (n + 1) * N_TILE)
-            acc = psum_o.tile([P, N_TILE], F32)
-            nc.tensor.matmul(acc[:], lhsT=ones[:], rhs=bo_rows[:, n_cols], start=True, stop=True)
-            nc.vector.tensor_copy(out=bias[:, n_cols], in_=acc[:])
 
         grouped_of_block = {}
         codes_of_block = {}
@@ -221,6 +223,8 @@ def tile_multimodalmutualattention_pb_kernel(tc, f0, f1, wo, bo, out):
                 )
 
         for step in range(BLOCKS + PROJECT_LAG):
+            if step < N_TILES:
+                prepare_wo(step)
             if step < BLOCKS:
                 make_comb(step)
             if 0 <= step - QUANTISE_LAG < BLOCKS:

@@ -90,9 +90,12 @@ def tile_multimodalmutualattention_pb_kernel(tc, f0, f1, wo, bo, out):
                     )
             return tp
 
-        def keep_transposed_head(tp):
+        def keep_transposed_head(tp, on_vector=False):
             fT = ft_pool.tile([P, 2, TOKENS], BF16)
-            nc.scalar.copy(out=fT[:], in_=tp[:])
+            if on_vector:
+                nc.vector.tensor_copy(out=fT[:], in_=tp[:])
+            else:
+                nc.scalar.copy(out=fT[:], in_=tp[:])
             return fT
 
         def comb_group(fT, bank, j, jc):
@@ -105,14 +108,20 @@ def tile_multimodalmutualattention_pb_kernel(tc, f0, f1, wo, bo, out):
                 bank[:, j, :], lhsT=fT[:, 1, rows], rhs=fT[:, 0, cols], start=False, stop=True
             )
 
-        fT_of_head = {0: keep_transposed_head(transpose_head(0))}
+        fT_of_head = {0: keep_transposed_head(transpose_head(0), on_vector=True)}
 
         bias = const.tile([P, FEATURES], F32)
-        for n in range(N_TILES):
-            n_cols = slice(n * N_TILE, (n + 1) * N_TILE)
+        bias_banks = {}
+
+        def spread_bias(n):
             acc = psum_o.tile([P, N_TILE], F32)
-            nc.tensor.matmul(acc[:], lhsT=ones[:], rhs=bo_rows[:, n_cols], start=True, stop=True)
-            nc.vector.tensor_copy(out=bias[:, n_cols], in_=acc[:])
+            nc.tensor.matmul(
+                acc[:], lhsT=ones[:], rhs=bo_rows[:, n * N_TILE : (n + 1) * N_TILE], start=True, stop=True
+            )
+            bias_banks[n] = acc
+
+        def keep_bias(n):
+            nc.scalar.copy(out=bias[:, n * N_TILE : (n + 1) * N_TILE], in_=bias_banks[n][:])
 
         wo_words = wo_sb[:].bitcast(F32).rearrange("r (b p u) -> r b u p", b=WO_ROW_TILES, u=WORDS)
         wo_grouped = const.tile([P, FEATURES * PACK], BF16, align_bytes=64)
@@ -123,7 +132,7 @@ def tile_multimodalmutualattention_pb_kernel(tc, f0, f1, wo, bo, out):
         wo_scales = const.tile([P, FEATURES], U8, align_bytes=64)
         tiles_per_bank = N_TILE // (WORDS * P)
 
-        def prepare_wo(n):
+        def transpose_wo(n):
             for first_b in range(n * tiles_per_half, (n + 1) * tiles_per_half, tiles_per_bank):
                 bank = psum_c.tile([P, tiles_per_bank, WORDS, P], F32, tag="bank")
                 for i in range(tiles_per_bank):
@@ -131,10 +140,18 @@ def tile_multimodalmutualattention_pb_kernel(tc, f0, f1, wo, bo, out):
                         nc.tensor.transpose(
                             bank[:, i, u, :], wo_words[:, first_b + i, u, :], ident_f32[:]
                         )
-                nc.vector.tensor_copy(
-                    out=wo_grouped_words[:, first_b : first_b + tiles_per_bank, :, :],
-                    in_=bank[:].rearrange("p i u r -> p i r u"),
-                )
+                if (first_b // tiles_per_bank) % 2 == 0:
+                    nc.vector.tensor_copy(
+                        out=wo_grouped_words[:, first_b : first_b + tiles_per_bank, :, :],
+                        in_=bank[:].rearrange("p i u r -> p i r u"),
+                    )
+                else:
+                    nc.scalar.copy(
+                        out=wo_grouped_words[:, first_b : first_b + tiles_per_bank, :, :],
+                        in_=bank[:].rearrange("p i u r -> p i r u"),
+                    )
+
+        def quantise_wo(n):
             nc.vector.quantize_mx(
                 out=wo_codes[:, n * N_TILE : (n + 1) * N_TILE].bitcast(FP8X4),
                 scales=wo_scales[:, n * N_TILE : (n + 1) * N_TILE],
@@ -146,7 +163,7 @@ def tile_multimodalmutualattention_pb_kernel(tc, f0, f1, wo, bo, out):
         scales_of_block = {}
         result_of_store = {}
 
-        def make_comb(block):
+        def make_comb(block, on_vector=False):
             h, jc = divmod(block, PACK)
             fT = fT_of_head[h]
             bank = psum_c.tile([P, PACK, P], F32, tag="bank")
@@ -166,7 +183,7 @@ def tile_multimodalmutualattention_pb_kernel(tc, f0, f1, wo, bo, out):
             )
             grouped_of_block[block] = grouped
             if transposes_here:
-                fT_of_head[h + 1] = keep_transposed_head(tp)
+                fT_of_head[h + 1] = keep_transposed_head(tp, on_vector)
 
         def quantise(block):
             codes = mx_pool.tile([P, P], U32, align_bytes=64)
@@ -222,9 +239,21 @@ def tile_multimodalmutualattention_pb_kernel(tc, f0, f1, wo, bo, out):
                     in_=result[:],
                 )
 
-        for step in range(BLOCKS + PROJECT_LAG):
-            if step < N_TILES:
-                prepare_wo(step)
+        transpose_wo(0)
+        make_comb(0)
+        quantise_wo(0)
+        spread_bias(1)
+        spread_bias(0)
+        transpose_wo(1)
+        quantise(0)
+        keep_bias(1)
+        quantise_wo(1)
+        make_comb(1, on_vector=True)
+        keep_bias(0)
+        make_comb(2)
+        quantise(1)
+        project(0)
+        for step in range(3, BLOCKS + PROJECT_LAG):
             if step < BLOCKS:
                 make_comb(step)
             if 0 <= step - QUANTISE_LAG < BLOCKS:

@@ -62,8 +62,10 @@ def tile_multimodalmutualattention_pb_kernel(tc, f0, f1, wo, bo, out):
         def load_heads(first, last):
             for f_dram, f_tile in zip((f0, f1), f_sb):
                 nc.sync.dma_start(
-                    out=f_tile[:, first:last, :],
-                    in_=f_dram[0, first:last].rearrange("h (p j) d -> p h (j d)", j=PACK),
+                    out=f_tile[:, first:last, :].rearrange("p h (u x) -> p (h u) x", u=WORDS),
+                    in_=f_dram[0, first:last].rearrange(
+                        "h (u p e) d -> p (h u) (e d)", u=WORDS, e=PACK // WORDS
+                    ),
                 )
 
         wo_sb = const.tile([P, WO_ROW_TILES * TOKENS], BF16)
@@ -123,7 +125,7 @@ def tile_multimodalmutualattention_pb_kernel(tc, f0, f1, wo, bo, out):
         def keep_bias(n):
             nc.scalar.copy(out=bias[:, n * N_TILE : (n + 1) * N_TILE], in_=bias_banks[n][:])
 
-        wo_words = wo_sb[:].bitcast(F32).rearrange("r (b p u) -> r b u p", b=WO_ROW_TILES, u=WORDS)
+        wo_words = wo_sb[:].bitcast(F32).rearrange("r (b u p) -> r b u p", b=WO_ROW_TILES, u=WORDS)
         wo_grouped = const.tile([P, FEATURES * PACK], BF16, align_bytes=64)
         wo_grouped_words = wo_grouped[:].bitcast(F32).rearrange(
             "p (b r u) -> p b r u", b=WO_ROW_TILES, u=WORDS
@@ -233,17 +235,17 @@ def tile_multimodalmutualattention_pb_kernel(tc, f0, f1, wo, bo, out):
             if place == BLOCKS_PER_STORE - 1:
                 first_jc = jc - place
                 nc.sync.dma_start(
-                    out=out[0, h].rearrange("(c j) d -> c j d", j=PACK)[
-                        :, first_jc : first_jc + BLOCKS_PER_STORE, :
+                    out=out[0, h].rearrange("(u c e) d -> c u e d", u=WORDS, e=PACK // WORDS)[
+                        :, first_jc // WORDS, first_jc % WORDS, :
                     ],
-                    in_=result[:],
+                    in_=result[:, 0, :],
                 )
 
+        spread_bias(1)
+        spread_bias(0)
         transpose_wo(0)
         make_comb(0)
         quantise_wo(0)
-        spread_bias(1)
-        spread_bias(0)
         transpose_wo(1)
         quantise(0)
         keep_bias(1)

@@ -30,6 +30,7 @@ assert PROJECT_LAG >= N_TILES
 TRANSPOSE_AT = 1
 
 BANKS_PER_DETOUR = 4
+WARM_UPS = 5
 
 FLOPS = 2 * HEADS * TOKENS * TOKENS * (2 * HEAD_DIM + FEATURES)
 
@@ -46,6 +47,11 @@ def tile_multimodalmutualattention_pb_kernel(tc, f0, f1, wo, bo, out):
         psum_o = ctx.enter_context(tc.psum_pool(name="psum_o", bufs=4))
         ctx.enter_context(tc.manual_schedule())
 
+        warm = const.tile([P, N_TILE], BF16)
+        nc.gpsimd.memset(warm[:], 0.0)
+        for i in range(WARM_UPS):
+            acc = psum_o.tile([P, N_TILE], F32)
+            nc.tensor.matmul(acc[:], lhsT=warm[:, 0:P], rhs=warm[:], start=True, stop=True)
         ident_bf16 = const.tile([P, P], BF16)
         make_identity(nc, ident_bf16[:])
         ident_f32 = const.tile([P, P], F32)

@@ -31,6 +31,7 @@ TRANSPOSE_AT = 1
 
 BANKS_PER_DETOUR = 4
 WARM_UPS = 5
+WO_TILES_PER_LOAD = 2
 
 FLOPS = 2 * HEADS * TOKENS * TOKENS * (2 * HEAD_DIM + FEATURES)
 
@@ -76,14 +77,19 @@ def tile_multimodalmutualattention_pb_kernel(tc, f0, f1, wo, bo, out):
 
         wo_sb = const.tile([P, WO_ROW_TILES * TOKENS], BF16)
         wo_sb_tiles = wo_sb[:].rearrange("r (b t) -> r b t", t=TOKENS)
-        wo_dram_tiles = wo.rearrange("(b r) t -> r b t", r=P)
+        wo_dram_tiles = wo.rearrange("(n r b) t -> r n b t", n=N_TILES, r=P)
         tiles_per_half = WO_ROW_TILES // N_TILES
 
         load_heads(0, 1)
         nc.sync.dma_start(out=bo_rows[0:1, :], in_=bo.rearrange("(o d) -> o d", o=1))
         for n in range(N_TILES):
-            b_range = slice(n * tiles_per_half, (n + 1) * tiles_per_half)
-            nc.sync.dma_start(out=wo_sb_tiles[:, b_range, :], in_=wo_dram_tiles[:, b_range, :])
+            for b in range(0, tiles_per_half, WO_TILES_PER_LOAD):
+                nc.sync.dma_start(
+                    out=wo_sb_tiles[
+                        :, n * tiles_per_half + b : n * tiles_per_half + b + WO_TILES_PER_LOAD, :
+                    ],
+                    in_=wo_dram_tiles[:, n, b : b + WO_TILES_PER_LOAD, :],
+                )
         load_heads(1, 2)
         load_heads(2, HEADS)
 
@@ -134,7 +140,7 @@ def tile_multimodalmutualattention_pb_kernel(tc, f0, f1, wo, bo, out):
         wo_words = wo_sb[:].bitcast(F32).rearrange("r (b u p) -> r b u p", b=WO_ROW_TILES, u=WORDS)
         wo_grouped = const.tile([P, FEATURES * PACK], BF16, align_bytes=64)
         wo_grouped_words = wo_grouped[:].bitcast(F32).rearrange(
-            "p (b r u) -> p b r u", b=WO_ROW_TILES, u=WORDS
+            "p (n r b u) -> p n r b u", n=N_TILES, r=P, u=WORDS
         )
         wo_codes = const.tile([P, FEATURES], U32, align_bytes=64)
         wo_scales = const.tile([P, FEATURES], U8, align_bytes=64)
@@ -142,6 +148,7 @@ def tile_multimodalmutualattention_pb_kernel(tc, f0, f1, wo, bo, out):
 
         def transpose_wo(n):
             for first_b in range(n * tiles_per_half, (n + 1) * tiles_per_half, tiles_per_bank):
+                in_half = first_b - n * tiles_per_half
                 bank = psum_c.tile([P, tiles_per_bank, WORDS, P], F32, tag="bank")
                 for i in range(tiles_per_bank):
                     for u in range(WORDS):
@@ -150,13 +157,13 @@ def tile_multimodalmutualattention_pb_kernel(tc, f0, f1, wo, bo, out):
                         )
                 if (first_b // tiles_per_bank) % 2 == 0:
                     nc.vector.tensor_copy(
-                        out=wo_grouped_words[:, first_b : first_b + tiles_per_bank, :, :],
-                        in_=bank[:].rearrange("p i u r -> p i r u"),
+                        out=wo_grouped_words[:, n, :, in_half : in_half + tiles_per_bank, :],
+                        in_=bank[:].rearrange("p i u r -> p r i u"),
                     )
                 else:
                     nc.scalar.copy(
-                        out=wo_grouped_words[:, first_b : first_b + tiles_per_bank, :, :],
-                        in_=bank[:].rearrange("p i u r -> p i r u"),
+                        out=wo_grouped_words[:, n, :, in_half : in_half + tiles_per_bank, :],
+                        in_=bank[:].rearrange("p i u r -> p r i u"),
                     )
 
         def quantise_wo(n):
@@ -204,6 +211,17 @@ def tile_multimodalmutualattention_pb_kernel(tc, f0, f1, wo, bo, out):
             codes_of_block[block] = codes
             scales_of_block[block] = scales
 
+        late_stores = []
+
+        def store_rows(what):
+            sh, sjc, sresult, cols = what
+            nc.sync.dma_start(
+                out=out[0, sh].rearrange("(u c e) d -> c u e d", u=WORDS, e=PACK // WORDS)[
+                    :, sjc // WORDS, sjc % WORDS, cols
+                ],
+                in_=sresult[:, 0, cols],
+            )
+
         def project(block):
             h, jc = divmod(block, PACK)
             store, place = divmod(block, BLOCKS_PER_STORE)
@@ -238,14 +256,21 @@ def tile_multimodalmutualattention_pb_kernel(tc, f0, f1, wo, bo, out):
                         in1=bias[:, n_cols],
                         op=mybir.AluOpType.add,
                     )
-            if place == BLOCKS_PER_STORE - 1:
-                first_jc = jc - place
-                nc.sync.dma_start(
-                    out=out[0, h].rearrange("(u c e) d -> c u e d", u=WORDS, e=PACK // WORDS)[
-                        :, first_jc // WORDS, first_jc % WORDS, :
-                    ],
-                    in_=result[:, 0, :],
-                )
+                if block >= 20 and block % 2 == 0:
+                    if n == 0:
+                        late_stores.append((h, jc, result, n_cols))
+                    else:
+                        store_rows((h, jc, result, n_cols))
+                elif block == BLOCKS - 1:
+                    store_rows((h, jc, result, n_cols))
+                    for late in late_stores:
+                        store_rows(late)
+                    late_stores.clear()
+            if (block < 20 or block % 2 == 1) and block < BLOCKS - 1:
+                store_rows((h, jc, result, slice(0, FEATURES)))
+                for late in late_stores:
+                    store_rows(late)
+                late_stores.clear()
 
         spread_bias(1)
         spread_bias(0)

@@ -229,6 +229,7 @@ def tile_multimodalmutualattention_pb_kernel(tc, f0, f1, wo, bo, out):
                 result = out_pool.tile([P, BLOCKS_PER_STORE, FEATURES], F32)
                 result_of_store[store] = result
             result = result_of_store[store]
+            has_detour = block % 2 == 0 and block % 8 != 4
             for n in range(N_TILES):
                 n_cols = slice(n * N_TILE, (n + 1) * N_TILE)
                 acc = psum_o.tile([P, N_TILE], F32)
@@ -241,7 +242,7 @@ def tile_multimodalmutualattention_pb_kernel(tc, f0, f1, wo, bo, out):
                     start=True,
                     stop=True,
                 )
-                if (block * N_TILES + n) % BANKS_PER_DETOUR == 0:
+                if has_detour and n == 0:
                     nc.scalar.copy(out=result[:, place, n_cols], in_=acc[:])
                     nc.gpsimd.tensor_tensor(
                         out=result[:, place, n_cols],
@@ -256,18 +257,21 @@ def tile_multimodalmutualattention_pb_kernel(tc, f0, f1, wo, bo, out):
                         in1=bias[:, n_cols],
                         op=mybir.AluOpType.add,
                     )
-                if block >= 20 and block % 2 == 0:
-                    if n == 0:
+                if block >= 20 and (has_detour or block == BLOCKS - 1):
+                    if has_detour and n == 0:
                         late_stores.append((h, jc, result, n_cols))
                     else:
+                        older = late_stores[: len(late_stores) - (1 if has_detour else 0)]
                         store_rows((h, jc, result, n_cols))
-                elif block == BLOCKS - 1:
-                    store_rows((h, jc, result, n_cols))
-                    for late in late_stores:
-                        store_rows(late)
-                    late_stores.clear()
-            if (block < 20 or block % 2 == 1) and block < BLOCKS - 1:
+                        for late in older:
+                            store_rows(late)
+                            late_stores.remove(late)
+            if block < 20 or not (has_detour or block == BLOCKS - 1):
                 store_rows((h, jc, result, slice(0, FEATURES)))
+                for late in late_stores:
+                    store_rows(late)
+                late_stores.clear()
+            if block == BLOCKS - 1:
                 for late in late_stores:
                     store_rows(late)
                 late_stores.clear()

import math
from contextlib import ExitStack

import concourse.mybir as mybir
from concourse.masks import make_identity

BF16 = mybir.dt.bfloat16
F32 = mybir.dt.float32
U32 = mybir.dt.uint32
U8 = mybir.dt.uint8
FP8X4 = mybir.dt.float8_e4m3fn_x4

P = 128
PACK = 4
HEADS = 8
TOKENS = 512
HEAD_DIM = 128
FEATURES = 1024
N_TILE = 512
N_TILES = FEATURES // N_TILE
WO_ROW_TILES = FEATURES // P
WORDS = 2
BLOCKS = HEADS * PACK
BLOCKS_PER_STORE = 1
COMB_SCALE = 0.5 / math.sqrt(HEAD_DIM)

QUANTISE_LAG = 1
PROJECT_LAG = 2
assert PROJECT_LAG >= N_TILES
TRANSPOSE_AT = 1

BANKS_PER_DETOUR = 4
WARM_UPS = 5
WO_TILES_PER_LOAD = 2

FLOPS = 2 * HEADS * TOKENS * TOKENS * (2 * HEAD_DIM + FEATURES)


def tile_multimodalmutualattention_pb_kernel(tc, f0, f1, wo, bo, out):
    nc = tc.nc
    with ExitStack() as ctx:
        const = ctx.enter_context(tc.tile_pool(name="const", bufs=1))
        ft_pool = ctx.enter_context(tc.tile_pool(name="ft", bufs=2))
        mx_pool = ctx.enter_context(tc.tile_pool(name="mx", bufs=4))
        out_pool = ctx.enter_context(tc.tile_pool(name="outs", bufs=6))
        psum_t = ctx.enter_context(tc.psum_pool(name="psum_t", bufs=1))
        psum_c = ctx.enter_context(tc.psum_pool(name="psum_c", bufs=3))
        psum_o = ctx.enter_context(tc.psum_pool(name="psum_o", bufs=4))
        ctx.enter_context(tc.manual_schedule())

        warm = const.tile([P, N_TILE], BF16)
        nc.gpsimd.memset(warm[:], 0.0)
        for i in range(WARM_UPS):
            acc = psum_o.tile([P, N_TILE], F32)
            nc.tensor.matmul(acc[:], lhsT=warm[:, 0:P], rhs=warm[:], start=True, stop=True)
        ident_bf16 = const.tile([P, P], BF16)
        make_identity(nc, ident_bf16[:])
        ident_f32 = const.tile([P, P], F32)
        make_identity(nc, ident_f32[:])
        bo_rows = const.tile([P, FEATURES], BF16)
        nc.vector.memset(bo_rows[:], 0.0)
        ones = const.tile([P, P], BF16)
        nc.vector.memset(ones[:], 1.0)

        f0_sb = const.tile([P, HEADS, PACK * HEAD_DIM], BF16)
        f1_sb = const.tile([P, HEADS, PACK * HEAD_DIM], BF16)
        f_sb = (f0_sb, f1_sb)

        def load_heads(first, last):
            for f_dram, f_tile in zip((f0, f1), f_sb):
                nc.sync.dma_start(
                    out=f_tile[:, first:last, :].rearrange("p h (u x) -> p (h u) x", u=WORDS),
                    in_=f_dram[0, first:last].rearrange(
                        "h (u p e) d -> p (h u) (e d)", u=WORDS, e=PACK // WORDS
                    ),
                )

        wo_sb = const.tile([P, WO_ROW_TILES * TOKENS], BF16)
        wo_sb_tiles = wo_sb[:].rearrange("r (b t) -> r b t", t=TOKENS)
        wo_dram_tiles = wo.rearrange("(n r b) t -> r n b t", n=N_TILES, r=P)
        tiles_per_half = WO_ROW_TILES // N_TILES

        load_heads(0, 1)
        nc.sync.dma_start(out=bo_rows[0:1, :], in_=bo.rearrange("(o d) -> o d", o=1))
        for n in range(N_TILES):
            for b in range(0, tiles_per_half, WO_TILES_PER_LOAD):
                nc.sync.dma_start(
                    out=wo_sb_tiles[
                        :, n * tiles_per_half + b : n * tiles_per_half + b + WO_TILES_PER_LOAD, :
                    ],
                    in_=wo_dram_tiles[:, n, b : b + WO_TILES_PER_LOAD, :],
                )
        load_heads(1, 2)
        load_heads(2, HEADS)

        def transpose_head(h):
            tp = psum_t.tile([P, 2, TOKENS], BF16)
            for source in range(2):
                for j in range(PACK):
                    nc.tensor.transpose(
                        tp[:, source, j * P : (j + 1) * P],
                        f_sb[source][:, h, j * HEAD_DIM : (j + 1) * HEAD_DIM],
                        ident_bf16[:],
                    )
            return tp

        def keep_transposed_head(tp, on_vector=False):
            fT = ft_pool.tile([P, 2, TOKENS], BF16)
            if on_vector:
                nc.vector.tensor_copy(out=fT[:], in_=tp[:])
            else:
                nc.scalar.copy(out=fT[:], in_=tp[:])
            return fT

        def comb_group(fT, bank, j, jc):
            rows = slice(j * P, (j + 1) * P)
            cols = slice(jc * P, (jc + 1) * P)
            nc.tensor.matmul(
                bank[:, j, :], lhsT=fT[:, 0, rows], rhs=fT[:, 1, cols], start=True, stop=False
            )
            nc.tensor.matmul(
                bank[:, j, :], lhsT=fT[:, 1, rows], rhs=fT[:, 0, cols], start=False, stop=True
            )

        fT_of_head = {0: keep_transposed_head(transpose_head(0), on_vector=True)}

        bias = const.tile([P, FEATURES], F32)
        bias_banks = {}

        def spread_bias(n):
            acc = psum_o.tile([P, N_TILE], F32)
            nc.tensor.matmul(
                acc[:], lhsT=ones[:], rhs=bo_rows[:, n * N_TILE : (n + 1) * N_TILE], start=True, stop=True
            )
            bias_banks[n] = acc

        def keep_bias(n):
            nc.scalar.copy(out=bias[:, n * N_TILE : (n + 1) * N_TILE], in_=bias_banks[n][:])

        wo_words = wo_sb[:].bitcast(F32).rearrange("r (b u p) -> r b u p", b=WO_ROW_TILES, u=WORDS)
        wo_grouped = const.tile([P, FEATURES * PACK], BF16, align_bytes=64)
        wo_grouped_words = wo_grouped[:].bitcast(F32).rearrange(
            "p (n r b u) -> p n r b u", n=N_TILES, r=P, u=WORDS
        )
        wo_codes = const.tile([P, FEATURES], U32, align_bytes=64)
        wo_scales = const.tile([P, FEATURES], U8, align_bytes=64)
        tiles_per_bank = N_TILE // (WORDS * P)

        def transpose_wo(n):
            for first_b in range(n * tiles_per_half, (n + 1) * tiles_per_half, tiles_per_bank):
                in_half = first_b - n * tiles_per_half
                bank = psum_c.tile([P, tiles_per_bank, WORDS, P], F32, tag="bank")
                for i in range(tiles_per_bank):
                    for u in range(WORDS):
                        nc.tensor.transpose(
                            bank[:, i, u, :], wo_words[:, first_b + i, u, :], ident_f32[:]
                        )
                if (first_b // tiles_per_bank) % 2 == 0:
                    nc.vector.tensor_copy(
                        out=wo_grouped_words[:, n, :, in_half : in_half + tiles_per_bank, :],
                        in_=bank[:].rearrange("p i u r -> p r i u"),
                    )
                else:
                    nc.scalar.copy(
                        out=wo_grouped_words[:, n, :, in_half : in_half + tiles_per_bank, :],
                        in_=bank[:].rearrange("p i u r -> p r i u"),
                    )

        def quantise_wo(n):
            nc.vector.quantize_mx(
                out=wo_codes[:, n * N_TILE : (n + 1) * N_TILE].bitcast(FP8X4),
                scales=wo_scales[:, n * N_TILE : (n + 1) * N_TILE],
                in_=wo_grouped[:, n * N_TILE * PACK : (n + 1) * N_TILE * PACK],
            )

        grouped_of_block = {}
        codes_of_block = {}
        scales_of_block = {}
        result_of_store = {}

        def make_comb(block, on_vector=False):
            h, jc = divmod(block, PACK)
            fT = fT_of_head[h]
            bank = psum_c.tile([P, PACK, P], F32, tag="bank")
            for j in range(PACK // 2):
                comb_group(fT, bank, j, jc)
            transposes_here = jc == TRANSPOSE_AT and h + 1 < HEADS
            if transposes_here:
                tp = transpose_head(h + 1)
            for j in range(PACK // 2, PACK):
                comb_group(fT, bank, j, jc)
            grouped = mx_pool.tile([P, P, PACK], BF16, align_bytes=64)
            nc.scalar.activation(
                out=grouped[:],
                in_=bank[:].rearrange("p j c -> p c j"),
                func=mybir.ActivationFunctionType.Copy,
                scale=COMB_SCALE,
            )
            grouped_of_block[block] = grouped
            if transposes_here:
                fT_of_head[h + 1] = keep_transposed_head(tp, on_vector)

        def quantise(block):
            codes = mx_pool.tile([P, P], U32, align_bytes=64)
            scales = mx_pool.tile([P, P], U8, align_bytes=64)
            nc.vector.quantize_mx(
                out=codes[:].bitcast(FP8X4),
                scales=scales[:],
                in_=grouped_of_block[block][:].rearrange("p c j -> p (c j)"),
            )
            codes_of_block[block] = codes
            scales_of_block[block] = scales

        late_stores = []

        def store_rows(what):
            sh, sjc, sresult, cols = what
            nc.sync.dma_start(
                out=out[0, sh].rearrange("(u c e) d -> c u e d", u=WORDS, e=PACK // WORDS)[
                    :, sjc // WORDS, sjc % WORDS, cols
                ],
                in_=sresult[:, 0, cols],
            )

        def project(block):
            h, jc = divmod(block, PACK)
            store, place = divmod(block, BLOCKS_PER_STORE)
            if place == 0:
                result = out_pool.tile([P, BLOCKS_PER_STORE, FEATURES], F32)
                result_of_store[store] = result
            result = result_of_store[store]
            has_detour = block % 2 == 0 and block % 8 != 4
            for n in range(N_TILES):
                n_cols = slice(n * N_TILE, (n + 1) * N_TILE)
                acc = psum_o.tile([P, N_TILE], F32)
                nc.tensor.matmul_mx(
                    out=acc[:],
                    lhsT=codes_of_block[block][:].bitcast(FP8X4),
                    lhsT_scale=scales_of_block[block][:],
                    rhs=wo_codes[:, n_cols].bitcast(FP8X4),
                    rhs_scale=wo_scales[:, n_cols],
                    start=True,
                    stop=True,
                )
                if has_detour and n == 0:
                    nc.scalar.copy(out=result[:, place, n_cols], in_=acc[:])
                    nc.gpsimd.tensor_tensor(
                        out=result[:, place, n_cols],
                        in0=result[:, place, n_cols],
                        in1=bias[:, n_cols],
                        op=mybir.AluOpType.add,
                    )
                else:
                    nc.vector.tensor_tensor(
                        out=result[:, place, n_cols],
                        in0=acc[:],
                        in1=bias[:, n_cols],
                        op=mybir.AluOpType.add,
                    )
                if block >= 20 and (has_detour or block == BLOCKS - 1):
                    if has_detour and n == 0:
                        late_stores.append((h, jc, result, n_cols))
                    else:
                        older = late_stores[: len(late_stores) - (1 if has_detour else 0)]
                        store_rows((h, jc, result, n_cols))
                        for late in older:
                            store_rows(late)
                            late_stores.remove(late)
            if block < 20 or not (has_detour or block == BLOCKS - 1):
                store_rows((h, jc, result, slice(0, FEATURES)))
                for late in late_stores:
                    store_rows(late)
                late_stores.clear()
            if block == BLOCKS - 1:
                for late in late_stores:
                    store_rows(late)
                late_stores.clear()

        spread_bias(1)
        spread_bias(0)
        transpose_wo(0)
        make_comb(0)
        quantise_wo(0)
        transpose_wo(1)
        quantise(0)
        keep_bias(1)
        quantise_wo(1)
        make_comb(1, on_vector=True)
        keep_bias(0)
        make_comb(2)
        quantise(1)
        project(0)
        for step in range(3, BLOCKS + PROJECT_LAG):
            if step < BLOCKS:
                make_comb(step)
            if 0 <= step - QUANTISE_LAG < BLOCKS:
                quantise(step - QUANTISE_LAG)
            if 0 <= step - PROJECT_LAG:
                project(step - PROJECT_LAG)
